import numpy as np
import ml_dtypes


def mxq(x, axis, fmt="e4m3"):
    dtype, down = {"e4m3": (ml_dtypes.float8_e4m3fn, 7), "e5m2": (ml_dtypes.float8_e5m2, 14)}[fmt]
    v = np.moveaxis(np.asarray(x, np.float32).astype(ml_dtypes.bfloat16).astype(np.float64), axis, -1)
    blocks = v.reshape(v.shape[:-1] + (-1, 32))
    amax = np.abs(blocks).max(-1, keepdims=True)
    byte = np.maximum(np.where(amax > 0, np.frexp(amax)[1] - 1 + 127, 0) - down, 1)
    scale = np.exp2(byte - 127.0)
    codes = (blocks / scale).astype(np.float32).astype(dtype).astype(np.float64)
    return np.moveaxis((codes * scale).reshape(v.shape), -1, axis)


WIDE = False


def mx_kscale(k):
    if not WIDE:
        return np.ones(k)
    levels = np.array([10, -10, 5, -5, 0])
    a = np.random.permutation(np.resize(levels, k // 512 * 4)).reshape(k // 512, 4)
    idx = np.arange(k)
    return np.exp2(a[idx // 512, idx % 128 // 32])


BF16 = ml_dtypes.bfloat16


def bf(x):
    return np.asarray(x, np.float32).astype(BF16)


def f64(x):
    return np.asarray(x).astype(np.float64)


E2M1 = np.array([0.0, 0.5, 1.0, 1.5, 2.0, 3.0, 4.0, 6.0, -0.0, -0.5, -1.0, -1.5, -2.0, -3.0, -4.0, -6.0])


def pack_weight(w, fmt):
    k, n = w.shape
    w = f64(bf(w)).reshape(k // 32, 32, n)
    amax = np.abs(w).max(1)
    if fmt == "e4m3":
        byte = np.frexp(amax)[1] - 1 + 127 - 7
    else:
        mant, ex = np.frexp(amax / 6.0)
        byte = np.where(mant > 0.5, ex, ex - 1) + 127
    byte = np.clip(np.where(amax > 0, byte, 1), 1, 254)
    scaled = (w * np.exp2(127.0 - byte)[:, None, :]).reshape(k, n).astype(np.float32)
    by_word = np.ascontiguousarray(scaled.reshape(k // 512, 128, 4, n).transpose(0, 1, 3, 2))
    if fmt == "e4m3":
        words = by_word.astype(ml_dtypes.float8_e4m3fn).view(np.uint8)
    else:
        c = by_word.astype(ml_dtypes.float4_e2m1fn).view(np.uint8) & 0xF
        words = c[..., 0::2] | (c[..., 1::2] << 4)
    return np.ascontiguousarray(words), np.ascontiguousarray(byte.astype(np.uint8).reshape(k // 512, 16, n))


def unpack_weight(words, scales, fmt):
    g, p, n, _ = words.shape
    if fmt == "e4m3":
        vals = np.ascontiguousarray(words).view(ml_dtypes.float8_e4m3fn).astype(np.float64)
    else:
        nib = np.empty((g, p, n, 4), np.uint8)
        nib[..., 0::2] = words & 0xF
        nib[..., 1::2] = words >> 4
        vals = E2M1[nib]
    vals = vals * np.repeat(np.exp2(scales.astype(np.float64) - 127.0), 8, axis=1)[..., None]
    return vals.transpose(0, 1, 3, 2).reshape(g * 512, n)

def pack4(w):
    words, scales = pack_weight(w, "e2m1")
    return words.reshape(words.shape[0], 128, -1), scales


def unpack4(words, scales):
    return unpack_weight(words.reshape(words.shape[0], 128, -1, 2), scales, "e2m1")


B, C, K, BK, BN = 1024, 2048, 2048, 1, 16
KEEP = 0.3


def setup_inputs():
    s = mx_kscale(C)
    x = np.random.standard_normal((B, C)) * s
    weight = np.random.uniform(-1.0, 1.0, (K, C)) * 3.2 / np.sqrt(C)
    blk = (np.random.uniform(0.0, 1.0, (K // BK, C // BN)) < KEEP).astype(np.float64)
    mask = np.repeat(np.repeat(blk, BK, axis=0), BN, axis=1)
    weight = weight * mask / s[None, :]
    bias = np.random.uniform(-1.0, 1.0, K) * 0.5
    words, scales = pack4(np.ascontiguousarray(weight.T))
    return {"x": bf(x), "weight_words": words, "weight_scales": scales, "bias": bf(bias)}


def reference(x, weight_words, weight_scales, bias):
    return np.maximum((mxq(f64(x), 1, "e4m3") @ unpack4(weight_words, weight_scales)) + f64(bias), 0.0)

@@ -1,0 +1,153 @@
+from contextlib import ExitStack
+
+import concourse.mybir as mybir
+from concourse.masks import make_identity
+
+F32 = mybir.dt.float32
+BF16 = mybir.dt.bfloat16
+I32 = mybir.dt.int32
+U32 = mybir.dt.uint32
+U8 = mybir.dt.uint8
+FP8X4 = mybir.dt.float8_e4m3fn_x4
+FP4X4 = mybir.dt.float4_e2m1fn_x4
+
+P = 128
+ROWS = 1024
+K = 2048
+N = 2048
+K_PASS = 4 * P
+GROUPS = K // K_PASS
+ROW_BLOCKS = ROWS // P
+BANK = 512
+COL_BLOCKS = N // BANK
+
+FLOPS = 2 * ROWS * K * N
+
+
+def tile_sparselinearrelu_kernel(tc, x, weight_words, weight_scales, bias, out):
+    nc = tc.nc
+    with ExitStack() as stack:
+        keep = stack.enter_context(tc.tile_pool(name="keep", bufs=1))
+        work = stack.enter_context(tc.tile_pool(name="work", bufs=3))
+        psum_t = stack.enter_context(tc.psum_pool(name="psum_t", bufs=2))
+        psum_o = stack.enter_context(tc.psum_pool(name="psum_o", bufs=6))
+        stack.enter_context(tc.manual_schedule())
+
+        w_words = keep.tile([P, GROUPS, 2 * N], U8, align_bytes=64)
+        w_planes = keep.tile([P, GROUPS, N], U8, align_bytes=64)
+        bias_all = keep.tile([P, N], BF16)
+        ident = keep.tile([P, P], F32)
+        warm = keep.tile([P, 1], F32)
+        x_raw = [keep.tile([P, K], BF16, name="x_raw%d" % i) for i in range(ROW_BLOCKS)]
+        x_codes = [
+            keep.tile([P, GROUPS * P], U32, name="x_codes%d" % i, align_bytes=64) for i in range(ROW_BLOCKS)
+        ]
+        x_planes = [
+            keep.tile([P, GROUPS * P], U8, name="x_planes%d" % i, align_bytes=64) for i in range(ROW_BLOCKS)
+        ]
+        grouped = {}
+
+        def load_x(i):
+            nc.sync.dma_start(out=x_raw[i][:], in_=x[i * P : (i + 1) * P, :])
+
+        nc.vector.memset(warm[:], 0.0)
+        nc.scalar.activation(out=warm[:], in_=warm[:], func=mybir.ActivationFunctionType.Relu)
+        for half in range(2):
+            nc.vector.memset(w_planes[:, 2 * half : 2 * half + 2, :].bitcast(I32), 0)
+        make_identity(nc, ident[:])
+
+        load_x(0)
+        load_x(1)
+        for half in range(2):
+            for b in range(2):
+                for r in range(4):
+                    nc.sync.dma_start(
+                        out=w_planes[32 * b + r : P : 64, 2 * half : 2 * half + 2, :].bitcast(I32),
+                        in_=weight_scales[2 * half : 2 * half + 2, 4 * b + r : 16 : 8, :]
+                        .rearrange("g q n -> q g n")
+                        .bitcast(I32),
+                    )
+        for g in range(GROUPS):
+            nc.sync.dma_start(out=w_words[:, g, :].bitcast(I32), in_=weight_words[g].bitcast(I32))
+        load_x(2)
+        nc.sync.dma_start(out=bias_all[:], in_=bias.partition_broadcast(P))
+        for i in range(3, ROW_BLOCKS):
+            load_x(i)
+
+        def transpose_block(i, copy_engines):
+            words = x_raw[i][:].bitcast(F32)
+            grouped[i] = work.tile([P, K], BF16, tag="grouped", name="grouped%d" % i, align_bytes=64)
+            pairs = grouped[i][:].bitcast(F32).rearrange("p (g m u) -> p g m u", g=GROUPS, u=2)
+            banks = []
+            for h in range(GROUPS // 2):
+                xt = psum_t.tile([P, 2, 2, P], F32, tag="xt")
+                banks.append(xt)
+                for gg in range(2):
+                    for u in range(2):
+                        first = (K_PASS // 2) * (2 * h + gg)
+                        nc.tensor.transpose(
+                            xt[:, gg, u, :], words[:, first + u : first + K_PASS // 2 : 2], ident[:]
+                        )
+            for h in range(GROUPS // 2):
+                copy_engines[h](
+                    out=pairs[:, 2 * h : 2 * h + 2, :, :], in_=banks[h][:].rearrange("p g u m -> p g m u")
+                )
+
+        def quantise(i, first_group, groups):
+            lo = first_group * P
+            hi = lo + groups * P
+            nc.vector.quantize_mx(
+                out=x_codes[i][:, lo:hi].bitcast(FP8X4),
+                scales=x_planes[i][:, lo:hi],
+                in_=grouped[i][:, 4 * lo : 4 * hi],
+            )
+
+        def one_pass(i, g, c, acc):
+            nc.tensor.matmul_mx(
+                out=acc[:],
+                lhsT=x_codes[i][:, g * P : (g + 1) * P].bitcast(FP8X4),
+                lhsT_scale=x_planes[i][:, g * P : (g + 1) * P],
+                rhs=w_words[:, g, 2 * BANK * c : 2 * BANK * (c + 1)].bitcast(FP4X4),
+                rhs_scale=w_planes[:, g, BANK * c : BANK * (c + 1)],
+                start=(g == 0),
+                stop=(g == GROUPS - 1),
+            )
+
+        def add_bias(c, acc, res):
+            cols = slice(BANK * c, BANK * (c + 1))
+            nc.vector.tensor_tensor(out=res[:, cols], in0=acc[:], in1=bias_all[:, cols], op=mybir.AluOpType.add)
+
+        def relu_store(i, c, res):
+            cols = slice(BANK * c, BANK * (c + 1))
+            nc.scalar.activation(out=res[:, cols], in_=res[:, cols], func=mybir.ActivationFunctionType.Relu)
+            if c % 2 == 1:
+                two = slice(BANK * (c - 1), BANK * (c + 1))
+                nc.scalar.dma_start(out=out[i * P : (i + 1) * P, two], in_=res[:, two])
+
+        transpose_block(0, [nc.vector.tensor_copy, nc.scalar.copy])
+        quantise(0, 0, 2)
+        quantise(0, 2, 2)
+        transpose_block(1, [nc.scalar.copy, nc.scalar.copy])
+        quantise(1, 0, GROUPS)
+
+        for i in range(ROW_BLOCKS):
+            res = work.tile([P, N], F32, tag="res")
+            if i == 0:
+                accs = [psum_o.tile([P, BANK], F32, tag="acc", name="acc0_%d" % c) for c in range(COL_BLOCKS)]
+                for g in range(GROUPS):
+                    for c in range(COL_BLOCKS):
+                        one_pass(i, g, c, accs[c])
+                for c in range(COL_BLOCKS):
+                    add_bias(c, accs[c], res)
+                    relu_store(i, c, res)
+            else:
+                for c in range(COL_BLOCKS):
+                    acc = psum_o.tile([P, BANK], F32, tag="acc")
+                    for g in range(GROUPS):
+                        one_pass(i, g, c, acc)
+                    add_bias(c, acc, res)
+                    if c == 0 and i + 1 < ROW_BLOCKS:
+                        quantise(i + 1, 0, GROUPS)
+                    relu_store(i, c, res)
+            if i + 2 < ROW_BLOCKS:
+                transpose_block(i + 2, [nc.scalar.copy, nc.scalar.copy])

@@ -26,16 +26,21 @@ FLOPS = 2 * ROWS * K * N
 
 def tile_sparselinearrelu_kernel(tc, x, weight_words, weight_scales, bias, out):
     nc = tc.nc
+    relu = mybir.ActivationFunctionType.Relu
     with ExitStack() as stack:
         keep = stack.enter_context(tc.tile_pool(name="keep", bufs=1))
-        work = stack.enter_context(tc.tile_pool(name="work", bufs=3))
-        psum_t = stack.enter_context(tc.psum_pool(name="psum_t", bufs=2))
-        psum_o = stack.enter_context(tc.psum_pool(name="psum_o", bufs=6))
+        work = stack.enter_context(tc.tile_pool(name="work", bufs=4))
+        psum_t = stack.enter_context(tc.psum_pool(name="psum_t", bufs=4))
+        psum_o = stack.enter_context(tc.psum_pool(name="psum_o", bufs=4))
         stack.enter_context(tc.manual_schedule())
 
-        w_words = keep.tile([P, GROUPS, 2 * N], U8, align_bytes=64)
+        w_words = [
+            keep.tile([P, GROUPS, 2 * BANK], U8, name="w_words%d" % c, align_bytes=64) for c in range(COL_BLOCKS)
+        ]
         w_planes = keep.tile([P, GROUPS, N], U8, align_bytes=64)
+        bias_row = keep.tile([P, N], BF16)
         bias_all = keep.tile([P, N], BF16)
+        ones = keep.tile([P, P], BF16)
         ident = keep.tile([P, P], F32)
         warm = keep.tile([P, 1], F32)
         x_raw = [keep.tile([P, K], BF16, name="x_raw%d" % i) for i in range(ROW_BLOCKS)]
@@ -45,109 +50,155 @@ def tile_sparselinearrelu_kernel(tc, x, weight_words, weight_scales, bias, out):
         x_planes = [
             keep.tile([P, GROUPS * P], U8, name="x_planes%d" % i, align_bytes=64) for i in range(ROW_BLOCKS)
         ]
+        x_sorted = {}
         grouped = {}
+        banks = {}
+        results = {}
 
         def load_x(i):
             nc.sync.dma_start(out=x_raw[i][:], in_=x[i * P : (i + 1) * P, :])
 
+        def load_w(c):
+            cols = slice(2 * BANK * c, 2 * BANK * (c + 1))
+            nc.sync.dma_start(
+                out=w_words[c][:].bitcast(I32),
+                in_=weight_words[:, :, cols].rearrange("g p b -> p g b").bitcast(I32),
+            )
+
         nc.vector.memset(warm[:], 0.0)
-        nc.scalar.activation(out=warm[:], in_=warm[:], func=mybir.ActivationFunctionType.Relu)
+        nc.scalar.activation(out=warm[:], in_=warm[:], func=relu)
         for half in range(2):
             nc.vector.memset(w_planes[:, 2 * half : 2 * half + 2, :].bitcast(I32), 0)
+        nc.vector.memset(bias_row[:].bitcast(I32), 0)
         make_identity(nc, ident[:])
+        nc.gpsimd.memset(ones[:], 1.0)
 
         load_x(0)
         load_x(1)
-        for half in range(2):
-            for b in range(2):
-                for r in range(4):
-                    nc.sync.dma_start(
-                        out=w_planes[32 * b + r : P : 64, 2 * half : 2 * half + 2, :].bitcast(I32),
-                        in_=weight_scales[2 * half : 2 * half + 2, 4 * b + r : 16 : 8, :]
-                        .rearrange("g q n -> q g n")
-                        .bitcast(I32),
-                    )
-        for g in range(GROUPS):
-            nc.sync.dma_start(out=w_words[:, g, :].bitcast(I32), in_=weight_words[g].bitcast(I32))
+        nc.scalar.dma_start(out=bias_row[0:1, :], in_=bias.rearrange("(o n) -> o n", o=1))
+        for b in range(2):
+            for r in range(4):
+                nc.sync.dma_start(
+                    out=w_planes[32 * b + r : P : 64, :, :].bitcast(I32),
+                    in_=weight_scales[:, 4 * b + r : 16 : 8, :].rearrange("g q n -> q g n").bitcast(I32),
+                )
+        load_w(0)
+        load_w(1)
         load_x(2)
-        nc.sync.dma_start(out=bias_all[:], in_=bias.partition_broadcast(P))
-        for i in range(3, ROW_BLOCKS):
+        load_w(2)
+        load_x(3)
+        load_w(3)
+        for i in range(4, ROW_BLOCKS):
             load_x(i)
 
-        def transpose_block(i, copy_engines):
-            words = x_raw[i][:].bitcast(F32)
-            grouped[i] = work.tile([P, K], BF16, tag="grouped", name="grouped%d" % i, align_bytes=64)
-            pairs = grouped[i][:].bitcast(F32).rearrange("p (g m u) -> p g m u", g=GROUPS, u=2)
-            banks = []
+        def sort_words(i):
+            x_sorted[i] = work.tile([P, K // 2], F32, tag="sorted", name="sorted%d" % i)
+            nc.vector.tensor_copy(
+                out=x_sorted[i][:].bitcast(I32).rearrange("p (g u c) -> p g u c", g=GROUPS, u=2),
+                in_=x_raw[i][:].bitcast(I32).rearrange("p (g c u) -> p g u c", g=GROUPS, u=2),
+            )
+
+        def transposes(i):
+            banks[i] = []
             for h in range(GROUPS // 2):
                 xt = psum_t.tile([P, 2, 2, P], F32, tag="xt")
-                banks.append(xt)
+                banks[i].append(xt)
                 for gg in range(2):
                     for u in range(2):
-                        first = (K_PASS // 2) * (2 * h + gg)
-                        nc.tensor.transpose(
-                            xt[:, gg, u, :], words[:, first + u : first + K_PASS // 2 : 2], ident[:]
-                        )
-            for h in range(GROUPS // 2):
-                copy_engines[h](
-                    out=pairs[:, 2 * h : 2 * h + 2, :, :], in_=banks[h][:].rearrange("p g u m -> p g m u")
-                )
+                        g = 2 * h + gg
+                        if i in x_sorted:
+                            src = x_sorted[i][:, (2 * g + u) * P : (2 * g + u + 1) * P]
+                        else:
+                            src = x_raw[i][:].bitcast(F32)[:, 2 * P * g + u : 2 * P * (g + 1) : 2]
+                        nc.tensor.transpose(xt[:, gg, u, :], src, ident[:])
+            grouped[i] = work.tile([P, K], BF16, tag="grouped", name="grouped%d" % i, align_bytes=64)
 
-        def quantise(i, first_group, groups):
-            lo = first_group * P
-            hi = lo + groups * P
+        def copy_out(i, h, copy):
+            pairs = grouped[i][:].bitcast(F32).rearrange("p (g m u) -> p g m u", g=GROUPS, u=2)
+            copy(out=pairs[:, 2 * h : 2 * h + 2, :, :], in_=banks[i][h][:].rearrange("p g u m -> p g m u"))
+
+        def quantise(i):
             nc.vector.quantize_mx(
-                out=x_codes[i][:, lo:hi].bitcast(FP8X4),
-                scales=x_planes[i][:, lo:hi],
-                in_=grouped[i][:, 4 * lo : 4 * hi],
+                out=x_codes[i][:].bitcast(FP8X4), scales=x_planes[i][:], in_=grouped[i][:]
             )
 
-        def one_pass(i, g, c, acc):
-            nc.tensor.matmul_mx(
-                out=acc[:],
-                lhsT=x_codes[i][:, g * P : (g + 1) * P].bitcast(FP8X4),
-                lhsT_scale=x_planes[i][:, g * P : (g + 1) * P],
-                rhs=w_words[:, g, 2 * BANK * c : 2 * BANK * (c + 1)].bitcast(FP4X4),
-                rhs_scale=w_planes[:, g, BANK * c : BANK * (c + 1)],
-                start=(g == 0),
-                stop=(g == GROUPS - 1),
+        def passes_and_bias(i, first, width):
+            acc = psum_o.tile([P, width], F32, tag="acc")
+            for g in range(GROUPS):
+                nc.tensor.matmul_mx(
+                    out=acc[:],
+                    lhsT=x_codes[i][:, g * P : (g + 1) * P].bitcast(FP8X4),
+                    lhsT_scale=x_planes[i][:, g * P : (g + 1) * P],
+                    rhs=w_words[first // BANK][:, g, 2 * (first % BANK) : 2 * (first % BANK + width)].bitcast(FP4X4),
+                    rhs_scale=w_planes[:, g, first : first + width],
+                    start=(g == 0),
+                    stop=(g == GROUPS - 1),
+                )
+            cols = slice(first, first + width)
+            nc.vector.tensor_tensor(
+                out=results[i][:, cols], in0=acc[:], in1=bias_all[:, cols], op=mybir.AluOpType.add
             )
 
-        def add_bias(c, acc, res):
-            cols = slice(BANK * c, BANK * (c + 1))
-            nc.vector.tensor_tensor(out=res[:, cols], in0=acc[:], in1=bias_all[:, cols], op=mybir.AluOpType.add)
+        def relu_store(i, first, width, store_first):
+            cols = slice(first, first + width)
+            nc.scalar.activation(out=results[i][:, cols], in_=results[i][:, cols], func=relu)
+            if store_first is not None:
+                span = slice(store_first, first + width)
+                nc.sync.dma_start(out=out[i * P : (i + 1) * P, span], in_=results[i][:, span])
 
-        def relu_store(i, c, res):
-            cols = slice(BANK * c, BANK * (c + 1))
-            nc.scalar.activation(out=res[:, cols], in_=res[:, cols], func=mybir.ActivationFunctionType.Relu)
-            if c % 2 == 1:
-                two = slice(BANK * (c - 1), BANK * (c + 1))
-                nc.scalar.dma_start(out=out[i * P : (i + 1) * P, two], in_=res[:, two])
+        transposes(0)
+        copy_out(0, 0, nc.vector.tensor_copy)
+        copy_out(0, 1, nc.scalar.copy)
+        quantise(0)
+        transposes(1)
+        copy_out(1, 0, nc.scalar.copy)
+        copy_out(1, 1, nc.vector.tensor_copy)
+        quantise(1)
+        for h in range(2):
+            spread = psum_t.tile([P, 2 * BANK], BF16, tag="xt")
+            for s in range(2):
+                cols = slice(BANK * (2 * h + s), BANK * (2 * h + s + 1))
+                nc.tensor.matmul(
+                    out=spread[:, BANK * s : BANK * (s + 1)], lhsT=ones[:], rhs=bias_row[:, cols], start=True, stop=True
+                )
+            copy = nc.scalar.copy if h == 0 else nc.vector.tensor_copy
+            copy(out=bias_all[:, 2 * BANK * h : 2 * BANK * (h + 1)], in_=spread[:])
 
-        transpose_block(0, [nc.vector.tensor_copy, nc.scalar.copy])
-        quantise(0, 0, 2)
-        quantise(0, 2, 2)
-        transpose_block(1, [nc.scalar.copy, nc.scalar.copy])
-        quantise(1, 0, GROUPS)
-
-        for i in range(ROW_BLOCKS):
-            res = work.tile([P, N], F32, tag="res")
-            if i == 0:
-                accs = [psum_o.tile([P, BANK], F32, tag="acc", name="acc0_%d" % c) for c in range(COL_BLOCKS)]
-                for g in range(GROUPS):
-                    for c in range(COL_BLOCKS):
-                        one_pass(i, g, c, accs[c])
-                for c in range(COL_BLOCKS):
-                    add_bias(c, accs[c], res)
-                    relu_store(i, c, res)
-            else:
-                for c in range(COL_BLOCKS):
-                    acc = psum_o.tile([P, BANK], F32, tag="acc")
-                    for g in range(GROUPS):
-                        one_pass(i, g, c, acc)
-                    add_bias(c, acc, res)
-                    if c == 0 and i + 1 < ROW_BLOCKS:
-                        quantise(i + 1, 0, GROUPS)
-                    relu_store(i, c, res)
-            if i + 2 < ROW_BLOCKS:
-                transpose_block(i + 2, [nc.scalar.copy, nc.scalar.copy])
+        for j in range(ROW_BLOCKS // 2):
+            a = 2 * j + 2
+            more = a < ROW_BLOCKS
+            for i in (2 * j, 2 * j + 1):
+                results[i] = work.tile([P, N], F32, tag="res", name="res%d" % i)
+            for idx in range(2 * COL_BLOCKS):
+                c = idx // 2
+                i = 2 * j + idx % 2
+                first = BANK * c
+                if not more and idx == 2 * COL_BLOCKS - 1:
+                    for q in range(4):
+                        passes_and_bias(i, first + P * q, P)
+                        relu_store(i, first + P * q, P, first + P * q)
+                    continue
+                passes_and_bias(i, first, BANK)
+                if not more and i == ROW_BLOCKS - 1 and c == 2:
+                    store_first = first
+                elif c % 2 == 1:
+                    store_first = first - BANK
+                else:
+                    store_first = None
+                if more and idx == 1:
+                    sort_words(a)
+                if more and idx == 3:
+                    sort_words(a + 1)
+                if more and idx == 5:
+                    transposes(a)
+                    transposes(a + 1)
+                    copy_out(a, 0, nc.scalar.copy)
+                    copy_out(a, 1, nc.scalar.copy)
+                    relu_store(i, first, BANK, store_first)
+                    copy_out(a + 1, 0, nc.scalar.copy)
+                    copy_out(a + 1, 1, nc.scalar.copy)
+                    quantise(a)
+                    continue
+                if more and idx == 6:
+                    quantise(a + 1)
+                relu_store(i, first, BANK, store_first)

@@ -37,7 +37,9 @@ def tile_sparselinearrelu_kernel(tc, x, weight_words, weight_scales, bias, out):
         w_words = [
             keep.tile([P, GROUPS, 2 * BANK], U8, name="w_words%d" % c, align_bytes=64) for c in range(COL_BLOCKS)
         ]
-        w_planes = keep.tile([P, GROUPS, N], U8, align_bytes=64)
+        w_planes = [
+            keep.tile([P, GROUPS, BANK], U8, name="w_planes%d" % c, align_bytes=64) for c in range(COL_BLOCKS)
+        ]
         bias_row = keep.tile([P, N], BF16)
         bias_all = keep.tile([P, N], BF16)
         ones = keep.tile([P, P], BF16)
@@ -65,28 +67,35 @@ def tile_sparselinearrelu_kernel(tc, x, weight_words, weight_scales, bias, out):
                 in_=weight_words[:, :, cols].rearrange("g p b -> p g b").bitcast(I32),
             )
 
+        def load_s(c):
+            cols = slice(BANK * c, BANK * (c + 1))
+            for r in range(4):
+                nc.sync.dma_start(
+                    out=w_planes[c][r:P:32, :, :].bitcast(I32),
+                    in_=weight_scales[:, r:16:4, cols].rearrange("g q n -> q g n").bitcast(I32),
+                )
+
         nc.vector.memset(warm[:], 0.0)
         nc.scalar.activation(out=warm[:], in_=warm[:], func=relu)
-        for half in range(2):
-            nc.vector.memset(w_planes[:, 2 * half : 2 * half + 2, :].bitcast(I32), 0)
+        nc.vector.memset(w_planes[0][:].bitcast(I32), 0)
         nc.vector.memset(bias_row[:].bitcast(I32), 0)
+        for c in range(1, COL_BLOCKS):
+            nc.vector.memset(w_planes[c][:].bitcast(I32), 0)
         make_identity(nc, ident[:])
         nc.gpsimd.memset(ones[:], 1.0)
 
         load_x(0)
         load_x(1)
         nc.scalar.dma_start(out=bias_row[0:1, :], in_=bias.rearrange("(o n) -> o n", o=1))
-        for b in range(2):
-            for r in range(4):
-                nc.sync.dma_start(
-                    out=w_planes[32 * b + r : P : 64, :, :].bitcast(I32),
-                    in_=weight_scales[:, 4 * b + r : 16 : 8, :].rearrange("g q n -> q g n").bitcast(I32),
-                )
+        load_s(0)
         load_w(0)
+        load_s(1)
         load_w(1)
         load_x(2)
+        load_s(2)
         load_w(2)
         load_x(3)
+        load_s(3)
         load_w(3)
         for i in range(4, ROW_BLOCKS):
             load_x(i)
@@ -130,7 +139,7 @@ def tile_sparselinearrelu_kernel(tc, x, weight_words, weight_scales, bias, out):
                     lhsT=x_codes[i][:, g * P : (g + 1) * P].bitcast(FP8X4),
                     lhsT_scale=x_planes[i][:, g * P : (g + 1) * P],
                     rhs=w_words[first // BANK][:, g, 2 * (first % BANK) : 2 * (first % BANK + width)].bitcast(FP4X4),
-                    rhs_scale=w_planes[:, g, first : first + width],
+                    rhs_scale=w_planes[first // BANK][:, g, first % BANK : first % BANK + width],
                     start=(g == 0),
                     stop=(g == GROUPS - 1),
                 )

@@ -45,7 +45,8 @@ def tile_sparselinearrelu_kernel(tc, x, weight_words, weight_scales, bias, out):
         ones = keep.tile([P, P], BF16)
         ident = keep.tile([P, P], F32)
         warm = keep.tile([P, 1], F32)
-        x_raw = [keep.tile([P, K], BF16, name="x_raw%d" % i) for i in range(ROW_BLOCKS)]
+        x_raw = [None] + [keep.tile([P, K], BF16, name="x_raw%d" % i) for i in range(1, ROW_BLOCKS)]
+        x_first = [keep.tile([P, K // 2], BF16, name="x_first%d" % h) for h in range(2)]
         x_codes = [
             keep.tile([P, GROUPS * P], U32, name="x_codes%d" % i, align_bytes=64) for i in range(ROW_BLOCKS)
         ]
@@ -84,7 +85,8 @@ def tile_sparselinearrelu_kernel(tc, x, weight_words, weight_scales, bias, out):
         make_identity(nc, ident[:])
         nc.gpsimd.memset(ones[:], 1.0)
 
-        load_x(0)
+        for h in range(2):
+            nc.sync.dma_start(out=x_first[h][:], in_=x[0:P, h * (K // 2) : (h + 1) * (K // 2)])
         load_x(1)
         nc.scalar.dma_start(out=bias_row[0:1, :], in_=bias.rearrange("(o n) -> o n", o=1))
         load_s(0)
@@ -117,6 +119,8 @@ def tile_sparselinearrelu_kernel(tc, x, weight_words, weight_scales, bias, out):
                         g = 2 * h + gg
                         if i in x_sorted:
                             src = x_sorted[i][:, (2 * g + u) * P : (2 * g + u + 1) * P]
+                        elif i == 0:
+                            src = x_first[h][:].bitcast(F32)[:, 2 * P * gg + u : 2 * P * (gg + 1) : 2]
                         else:
                             src = x_raw[i][:].bitcast(F32)[:, 2 * P * g + u : 2 * P * (g + 1) : 2]
                         nc.tensor.transpose(xt[:, gg, u, :], src, ident[:])
@@ -176,6 +180,7 @@ def tile_sparselinearrelu_kernel(tc, x, weight_words, weight_scales, bias, out):
         for j in range(ROW_BLOCKS // 2):
             a = 2 * j + 2
             more = a < ROW_BLOCKS
+            sort_at, run_at = ((1, 3), 5) if j == 0 else ((0, 1), 3)
             for i in (2 * j, 2 * j + 1):
                 results[i] = work.tile([P, N], F32, tag="res", name="res%d" % i)
             for idx in range(2 * COL_BLOCKS):
@@ -194,11 +199,11 @@ def tile_sparselinearrelu_kernel(tc, x, weight_words, weight_scales, bias, out):
                     store_first = first - BANK
                 else:
                     store_first = None
-                if more and idx == 1:
+                if more and idx == sort_at[0]:
                     sort_words(a)
-                if more and idx == 3:
+                if more and idx == sort_at[1]:
                     sort_words(a + 1)
-                if more and idx == 5:
+                if more and idx == run_at:
                     transposes(a)
                     transposes(a + 1)
                     copy_out(a, 0, nc.scalar.copy)
@@ -208,6 +213,6 @@ def tile_sparselinearrelu_kernel(tc, x, weight_words, weight_scales, bias, out):
                     copy_out(a + 1, 1, nc.scalar.copy)
                     quantise(a)
                     continue
-                if more and idx == 6:
+                if more and idx == run_at + 1:
                     quantise(a + 1)
                 relu_store(i, first, BANK, store_first)

@@ -35,7 +35,8 @@ def tile_sparselinearrelu_kernel(tc, x, weight_words, weight_scales, bias, out):
         stack.enter_context(tc.manual_schedule())
 
         w_words = [
-            keep.tile([P, GROUPS, 2 * BANK], U8, name="w_words%d" % c, align_bytes=64) for c in range(COL_BLOCKS)
+            [keep.tile([P, 2, 2 * BANK], U8, name="w_words%d_%d" % (c, h), align_bytes=64) for h in range(GROUPS // 2)]
+            for c in range(COL_BLOCKS)
         ]
         w_planes = [
             keep.tile([P, GROUPS, BANK], U8, name="w_planes%d" % c, align_bytes=64) for c in range(COL_BLOCKS)
@@ -63,10 +64,11 @@ def tile_sparselinearrelu_kernel(tc, x, weight_words, weight_scales, bias, out):
 
         def load_w(c):
             cols = slice(2 * BANK * c, 2 * BANK * (c + 1))
-            nc.sync.dma_start(
-                out=w_words[c][:].bitcast(I32),
-                in_=weight_words[:, :, cols].rearrange("g p b -> p g b").bitcast(I32),
-            )
+            for h in range(GROUPS // 2):
+                nc.sync.dma_start(
+                    out=w_words[c][h][:].bitcast(I32),
+                    in_=weight_words[2 * h : 2 * h + 2, :, cols].rearrange("g p b -> p g b").bitcast(I32),
+                )
 
         def load_s(c):
             cols = slice(BANK * c, BANK * (c + 1))
@@ -93,9 +95,9 @@ def tile_sparselinearrelu_kernel(tc, x, weight_words, weight_scales, bias, out):
         load_w(0)
         load_s(1)
         load_w(1)
-        load_x(2)
         load_s(2)
         load_w(2)
+        load_x(2)
         load_x(3)
         load_s(3)
         load_w(3)
@@ -142,7 +144,7 @@ def tile_sparselinearrelu_kernel(tc, x, weight_words, weight_scales, bias, out):
                     out=acc[:],
                     lhsT=x_codes[i][:, g * P : (g + 1) * P].bitcast(FP8X4),
                     lhsT_scale=x_planes[i][:, g * P : (g + 1) * P],
-                    rhs=w_words[first // BANK][:, g, 2 * (first % BANK) : 2 * (first % BANK + width)].bitcast(FP4X4),
+                    rhs=w_words[first // BANK][g // 2][:, g % 2, 2 * (first % BANK) : 2 * (first % BANK + width)].bitcast(FP4X4),
                     rhs_scale=w_planes[first // BANK][:, g, first % BANK : first % BANK + width],
                     start=(g == 0),
                     stop=(g == GROUPS - 1),
@@ -180,7 +182,7 @@ def tile_sparselinearrelu_kernel(tc, x, weight_words, weight_scales, bias, out):
         for j in range(ROW_BLOCKS // 2):
             a = 2 * j + 2
             more = a < ROW_BLOCKS
-            sort_at, run_at = ((1, 3), 5) if j == 0 else ((0, 1), 3)
+            sort_at, run_at = ((3, 4), 5) if j == 0 else ((0, 1), 3)
             for i in (2 * j, 2 * j + 1):
                 results[i] = work.tile([P, N], F32, tag="res", name="res%d" % i)
             for idx in range(2 * COL_BLOCKS):

@@ -192,7 +192,7 @@ def tile_sparselinearrelu_kernel(tc, x, weight_words, weight_scales, bias, out):
                 if not more and idx == 2 * COL_BLOCKS - 1:
                     for q in range(4):
                         passes_and_bias(i, first + P * q, P)
-                        relu_store(i, first + P * q, P, first + P * q)
+                        relu_store(i, first + P * q, P, first if q == 3 else None)
                     continue
                 passes_and_bias(i, first, BANK)
                 if not more and i == ROW_BLOCKS - 1 and c == 2:

@@ -186,8 +186,10 @@ def tile_sparselinearrelu_kernel(tc, x, weight_words, weight_scales, bias, out):
             for i in (2 * j, 2 * j + 1):
                 results[i] = work.tile([P, N], F32, tag="res", name="res%d" % i)
             for idx in range(2 * COL_BLOCKS):
-                c = idx // 2
-                i = 2 * j + idx % 2
+                if more:
+                    c, i = idx // 2, 2 * j + idx % 2
+                else:
+                    c, i = idx % COL_BLOCKS, 2 * j + idx // COL_BLOCKS
                 first = BANK * c
                 if not more and idx == 2 * COL_BLOCKS - 1:
                     for q in range(4):

@@ -21,6 +21,9 @@ ROW_BLOCKS = ROWS // P
 BANK = 512
 COL_BLOCKS = N // BANK
 
+X_PARTS = (2, 2, 1, 2, 1, 1, 1, 1)
+W_PARTS = (2, 2, 2, 4)
+
 FLOPS = 2 * ROWS * K * N
 
 
@@ -35,7 +38,10 @@ def tile_sparselinearrelu_kernel(tc, x, weight_words, weight_scales, bias, out):
         stack.enter_context(tc.manual_schedule())
 
         w_words = [
-            [keep.tile([P, 2, 2 * BANK], U8, name="w_words%d_%d" % (c, h), align_bytes=64) for h in range(GROUPS // 2)]
+            [
+                keep.tile([P, GROUPS // W_PARTS[c], 2 * BANK], U8, name="w_words%d_%d" % (c, h), align_bytes=64)
+                for h in range(W_PARTS[c])
+            ]
             for c in range(COL_BLOCKS)
         ]
         w_planes = [
@@ -46,8 +52,10 @@ def tile_sparselinearrelu_kernel(tc, x, weight_words, weight_scales, bias, out):
         ones = keep.tile([P, P], BF16)
         ident = keep.tile([P, P], F32)
         warm = keep.tile([P, 1], F32)
-        x_raw = [None] + [keep.tile([P, K], BF16, name="x_raw%d" % i) for i in range(1, ROW_BLOCKS)]
-        x_first = [keep.tile([P, K // 2], BF16, name="x_first%d" % h) for h in range(2)]
+        x_raw = [
+            [keep.tile([P, K // X_PARTS[i]], BF16, name="x_raw%d_%d" % (i, h)) for h in range(X_PARTS[i])]
+            for i in range(ROW_BLOCKS)
+        ]
         x_codes = [
             keep.tile([P, GROUPS * P], U32, name="x_codes%d" % i, align_bytes=64) for i in range(ROW_BLOCKS)
         ]
@@ -60,14 +68,17 @@ def tile_sparselinearrelu_kernel(tc, x, weight_words, weight_scales, bias, out):
         results = {}
 
         def load_x(i):
-            nc.sync.dma_start(out=x_raw[i][:], in_=x[i * P : (i + 1) * P, :])
+            width = K // X_PARTS[i]
+            for h in range(X_PARTS[i]):
+                nc.sync.dma_start(out=x_raw[i][h][:], in_=x[i * P : (i + 1) * P, h * width : (h + 1) * width])
 
         def load_w(c):
             cols = slice(2 * BANK * c, 2 * BANK * (c + 1))
-            for h in range(GROUPS // 2):
+            per = GROUPS // W_PARTS[c]
+            for h in range(W_PARTS[c]):
                 nc.sync.dma_start(
                     out=w_words[c][h][:].bitcast(I32),
-                    in_=weight_words[2 * h : 2 * h + 2, :, cols].rearrange("g p b -> p g b").bitcast(I32),
+                    in_=weight_words[per * h : per * (h + 1), :, cols].rearrange("g p b -> p g b").bitcast(I32),
                 )
 
         def load_s(c):
@@ -87,8 +98,7 @@ def tile_sparselinearrelu_kernel(tc, x, weight_words, weight_scales, bias, out):
         make_identity(nc, ident[:])
         nc.gpsimd.memset(ones[:], 1.0)
 
-        for h in range(2):
-            nc.sync.dma_start(out=x_first[h][:], in_=x[0:P, h * (K // 2) : (h + 1) * (K // 2)])
+        load_x(0)
         load_x(1)
         nc.scalar.dma_start(out=bias_row[0:1, :], in_=bias.rearrange("(o n) -> o n", o=1))
         load_s(0)
@@ -106,10 +116,15 @@ def tile_sparselinearrelu_kernel(tc, x, weight_words, weight_scales, bias, out):
 
         def sort_words(i):
             x_sorted[i] = work.tile([P, K // 2], F32, tag="sorted", name="sorted%d" % i)
-            nc.vector.tensor_copy(
-                out=x_sorted[i][:].bitcast(I32).rearrange("p (g u c) -> p g u c", g=GROUPS, u=2),
-                in_=x_raw[i][:].bitcast(I32).rearrange("p (g c u) -> p g u c", g=GROUPS, u=2),
-            )
+            per = GROUPS // X_PARTS[i]
+            words = K // 2 // X_PARTS[i]
+            for h in range(X_PARTS[i]):
+                nc.vector.tensor_copy(
+                    out=x_sorted[i][:, h * words : (h + 1) * words]
+                    .bitcast(I32)
+                    .rearrange("p (g u c) -> p g u c", g=per, u=2),
+                    in_=x_raw[i][h][:].bitcast(I32).rearrange("p (g c u) -> p g u c", g=per, u=2),
+                )
 
         def transposes(i):
             banks[i] = []
@@ -121,10 +136,8 @@ def tile_sparselinearrelu_kernel(tc, x, weight_words, weight_scales, bias, out):
                         g = 2 * h + gg
                         if i in x_sorted:
                             src = x_sorted[i][:, (2 * g + u) * P : (2 * g + u + 1) * P]
-                        elif i == 0:
-                            src = x_first[h][:].bitcast(F32)[:, 2 * P * gg + u : 2 * P * (gg + 1) : 2]
                         else:
-                            src = x_raw[i][:].bitcast(F32)[:, 2 * P * g + u : 2 * P * (g + 1) : 2]
+                            src = x_raw[i][h][:].bitcast(F32)[:, 2 * P * gg + u : 2 * P * (gg + 1) : 2]
                         nc.tensor.transpose(xt[:, gg, u, :], src, ident[:])
             grouped[i] = work.tile([P, K], BF16, tag="grouped", name="grouped%d" % i, align_bytes=64)
 
@@ -137,6 +150,10 @@ def tile_sparselinearrelu_kernel(tc, x, weight_words, weight_scales, bias, out):
                 out=x_codes[i][:].bitcast(FP8X4), scales=x_planes[i][:], in_=grouped[i][:]
             )
 
+        def w_part(c, g):
+            per = GROUPS // W_PARTS[c]
+            return w_words[c][g // per][:, g % per, :]
+
         def passes_and_bias(i, first, width):
             acc = psum_o.tile([P, width], F32, tag="acc")
             for g in range(GROUPS):
@@ -144,7 +161,7 @@ def tile_sparselinearrelu_kernel(tc, x, weight_words, weight_scales, bias, out):
                     out=acc[:],
                     lhsT=x_codes[i][:, g * P : (g + 1) * P].bitcast(FP8X4),
                     lhsT_scale=x_planes[i][:, g * P : (g + 1) * P],
-                    rhs=w_words[first // BANK][g // 2][:, g % 2, 2 * (first % BANK) : 2 * (first % BANK + width)].bitcast(FP4X4),
+                    rhs=w_part(first // BANK, g)[:, 2 * (first % BANK) : 2 * (first % BANK + width)].bitcast(FP4X4),
                     rhs_scale=w_planes[first // BANK][:, g, first % BANK : first % BANK + width],
                     start=(g == 0),
                     stop=(g == GROUPS - 1),

@@ -49,7 +49,7 @@ def tile_sparselinearrelu_kernel(tc, x, weight_words, weight_scales, bias, out):
         ]
         bias_row = keep.tile([P, N], BF16)
         bias_all = keep.tile([P, N], BF16)
-        ones = keep.tile([P, P], BF16)
+        ones = keep.tile([P, BANK], BF16)
         ident = keep.tile([P, P], F32)
         warm = keep.tile([P, 1], F32)
         x_raw = [
@@ -95,8 +95,8 @@ def tile_sparselinearrelu_kernel(tc, x, weight_words, weight_scales, bias, out):
         nc.vector.memset(bias_row[:].bitcast(I32), 0)
         for c in range(1, COL_BLOCKS):
             nc.vector.memset(w_planes[c][:].bitcast(I32), 0)
-        make_identity(nc, ident[:])
         nc.gpsimd.memset(ones[:], 1.0)
+        make_identity(nc, ident[:])
 
         load_x(0)
         load_x(1)
@@ -126,9 +126,14 @@ def tile_sparselinearrelu_kernel(tc, x, weight_words, weight_scales, bias, out):
                     in_=x_raw[i][h][:].bitcast(I32).rearrange("p (g c u) -> p g u c", g=per, u=2),
                 )
 
-        def transposes(i):
+        def warm_up(count):
+            for n in range(count):
+                nc.tensor.matmul(out=idle[:], lhsT=ones[:, :P], rhs=ones[:], start=True, stop=True)
+
+        def transposes(i, warm_ups=0):
             banks[i] = []
             for h in range(GROUPS // 2):
+                warm_up(warm_ups if h > 0 else 0)
                 xt = psum_t.tile([P, 2, 2, P], F32, tag="xt")
                 banks[i].append(xt)
                 for gg in range(2):
@@ -178,11 +183,14 @@ def tile_sparselinearrelu_kernel(tc, x, weight_words, weight_scales, bias, out):
                 span = slice(store_first, first + width)
                 nc.sync.dma_start(out=out[i * P : (i + 1) * P, span], in_=results[i][:, span])
 
-        transposes(0)
+        idle = psum_o.tile([P, BANK], F32, tag="acc")
+        warm_up(4)
+        transposes(0, 1)
+        warm_up(1)
         copy_out(0, 0, nc.vector.tensor_copy)
         copy_out(0, 1, nc.scalar.copy)
         quantise(0)
-        transposes(1)
+        transposes(1, 1)
         copy_out(1, 0, nc.scalar.copy)
         copy_out(1, 1, nc.vector.tensor_copy)
         quantise(1)
@@ -191,7 +199,7 @@ def tile_sparselinearrelu_kernel(tc, x, weight_words, weight_scales, bias, out):
             for s in range(2):
                 cols = slice(BANK * (2 * h + s), BANK * (2 * h + s + 1))
                 nc.tensor.matmul(
-                    out=spread[:, BANK * s : BANK * (s + 1)], lhsT=ones[:], rhs=bias_row[:, cols], start=True, stop=True
+                    out=spread[:, BANK * s : BANK * (s + 1)], lhsT=ones[:, :P], rhs=bias_row[:, cols], start=True, stop=True
                 )
             copy = nc.scalar.copy if h == 0 else nc.vector.tensor_copy
             copy(out=bias_all[:, 2 * BANK * h : 2 * BANK * (h + 1)], in_=spread[:])

@@ -47,7 +47,8 @@ def tile_sparselinearrelu_kernel(tc, x, weight_words, weight_scales, bias, out):
         w_planes = [
             keep.tile([P, GROUPS, BANK], U8, name="w_planes%d" % c, align_bytes=64) for c in range(COL_BLOCKS)
         ]
-        bias_row = keep.tile([P, N], BF16)
+        bias_rows = keep.tile([P, BANK], BF16)
+        pick = keep.tile([P, COL_BLOCKS], BF16)
         bias_all = keep.tile([P, N], BF16)
         ones = keep.tile([P, BANK], BF16)
         ident = keep.tile([P, P], F32)
@@ -89,18 +90,20 @@ def tile_sparselinearrelu_kernel(tc, x, weight_words, weight_scales, bias, out):
                     in_=weight_scales[:, r:16:4, cols].rearrange("g q n -> q g n").bitcast(I32),
                 )
 
+        nc.vector.memset(bias_rows[:].bitcast(I32), 0)
         nc.vector.memset(warm[:], 0.0)
         nc.scalar.activation(out=warm[:], in_=warm[:], func=relu)
         nc.vector.memset(w_planes[0][:].bitcast(I32), 0)
-        nc.vector.memset(bias_row[:].bitcast(I32), 0)
-        for c in range(1, COL_BLOCKS):
-            nc.vector.memset(w_planes[c][:].bitcast(I32), 0)
+        nc.vector.memset(w_planes[1][:].bitcast(I32), 0)
         nc.gpsimd.memset(ones[:], 1.0)
         make_identity(nc, ident[:])
+        nc.vector.tensor_copy(out=pick[:], in_=ident[:, :COL_BLOCKS])
+        for c in range(2, COL_BLOCKS):
+            nc.vector.memset(w_planes[c][:].bitcast(I32), 0)
 
         load_x(0)
+        nc.sync.dma_start(out=bias_rows[0:COL_BLOCKS, :], in_=bias.rearrange("(c n) -> c n", c=COL_BLOCKS))
         load_x(1)
-        nc.scalar.dma_start(out=bias_row[0:1, :], in_=bias.rearrange("(o n) -> o n", o=1))
         load_s(0)
         load_w(0)
         load_s(1)
@@ -126,14 +129,18 @@ def tile_sparselinearrelu_kernel(tc, x, weight_words, weight_scales, bias, out):
                     in_=x_raw[i][h][:].bitcast(I32).rearrange("p (g c u) -> p g u c", g=per, u=2),
                 )
 
-        def warm_up(count):
-            for n in range(count):
-                nc.tensor.matmul(out=idle[:], lhsT=ones[:, :P], rhs=ones[:], start=True, stop=True)
+        def spread_bias(c):
+            nc.tensor.matmul(
+                out=spread[c // 2][:, BANK * (c % 2) : BANK * (c % 2 + 1)],
+                lhsT=pick[:, c : c + 1].to_broadcast([P, P]),
+                rhs=bias_rows[:],
+                start=True,
+                stop=True,
+            )
 
-        def transposes(i, warm_ups=0):
+        def transposes(i):
             banks[i] = []
             for h in range(GROUPS // 2):
-                warm_up(warm_ups if h > 0 else 0)
                 xt = psum_t.tile([P, 2, 2, P], F32, tag="xt")
                 banks[i].append(xt)
                 for gg in range(2):
@@ -144,16 +151,23 @@ def tile_sparselinearrelu_kernel(tc, x, weight_words, weight_scales, bias, out):
                         else:
                             src = x_raw[i][h][:].bitcast(F32)[:, 2 * P * gg + u : 2 * P * (gg + 1) : 2]
                         nc.tensor.transpose(xt[:, gg, u, :], src, ident[:])
+                if i < 2:
+                    spread_bias(2 * i + h)
             grouped[i] = work.tile([P, K], BF16, tag="grouped", name="grouped%d" % i, align_bytes=64)
 
         def copy_out(i, h, copy):
             pairs = grouped[i][:].bitcast(F32).rearrange("p (g m u) -> p g m u", g=GROUPS, u=2)
             copy(out=pairs[:, 2 * h : 2 * h + 2, :, :], in_=banks[i][h][:].rearrange("p g u m -> p g m u"))
 
-        def quantise(i):
-            nc.vector.quantize_mx(
-                out=x_codes[i][:].bitcast(FP8X4), scales=x_planes[i][:], in_=grouped[i][:]
-            )
+        def quantise(i, parts=(0,), of=1):
+            width = GROUPS * P // of
+            for n in parts:
+                cols = slice(n * width, (n + 1) * width)
+                nc.vector.quantize_mx(
+                    out=x_codes[i][:, cols].bitcast(FP8X4),
+                    scales=x_planes[i][:, cols],
+                    in_=grouped[i][:, 4 * n * width : 4 * (n + 1) * width],
+                )
 
         def w_part(c, g):
             per = GROUPS // W_PARTS[c]
@@ -184,25 +198,21 @@ def tile_sparselinearrelu_kernel(tc, x, weight_words, weight_scales, bias, out):
                 nc.sync.dma_start(out=out[i * P : (i + 1) * P, span], in_=results[i][:, span])
 
         idle = psum_o.tile([P, BANK], F32, tag="acc")
-        warm_up(4)
-        transposes(0, 1)
-        warm_up(1)
+        for n in range(4):
+            nc.tensor.matmul(out=idle[:], lhsT=ones[:, :P], rhs=ones[:], start=True, stop=True)
+        spread = [psum_o.tile([P, 2 * BANK], BF16, tag="acc", name="spread%d" % h) for h in range(2)]
+        transposes(0)
         copy_out(0, 0, nc.vector.tensor_copy)
         copy_out(0, 1, nc.scalar.copy)
-        quantise(0)
-        transposes(1, 1)
+        quantise(0, (0, 1), 2)
+        transposes(1)
         copy_out(1, 0, nc.scalar.copy)
+        quantise(1, (0,), 2)
         copy_out(1, 1, nc.vector.tensor_copy)
-        quantise(1)
+        quantise(1, (1,), 2)
         for h in range(2):
-            spread = psum_t.tile([P, 2 * BANK], BF16, tag="xt")
-            for s in range(2):
-                cols = slice(BANK * (2 * h + s), BANK * (2 * h + s + 1))
-                nc.tensor.matmul(
-                    out=spread[:, BANK * s : BANK * (s + 1)], lhsT=ones[:, :P], rhs=bias_row[:, cols], start=True, stop=True
-                )
             copy = nc.scalar.copy if h == 0 else nc.vector.tensor_copy
-            copy(out=bias_all[:, 2 * BANK * h : 2 * BANK * (h + 1)], in_=spread[:])
+            copy(out=bias_all[:, 2 * BANK * h : 2 * BANK * (h + 1)], in_=spread[h][:])
 
         for j in range(ROW_BLOCKS // 2):
             a = 2 * j + 2
@@ -219,7 +229,7 @@ def tile_sparselinearrelu_kernel(tc, x, weight_words, weight_scales, bias, out):
                 if not more and idx == 2 * COL_BLOCKS - 1:
                     for q in range(4):
                         passes_and_bias(i, first + P * q, P)
-                        relu_store(i, first + P * q, P, first if q == 3 else None)
+                        relu_store(i, first + P * q, P, first + P * (q - 1) if q % 2 == 1 else None)
                     continue
                 passes_and_bias(i, first, BANK)
                 if not more and i == ROW_BLOCKS - 1 and c == 2:

from contextlib import ExitStack

import concourse.mybir as mybir
from concourse.masks import make_identity

F32 = mybir.dt.float32
BF16 = mybir.dt.bfloat16
I32 = mybir.dt.int32
U32 = mybir.dt.uint32
U8 = mybir.dt.uint8
FP8X4 = mybir.dt.float8_e4m3fn_x4
FP4X4 = mybir.dt.float4_e2m1fn_x4

P = 128
ROWS = 1024
K = 2048
N = 2048
K_PASS = 4 * P
GROUPS = K // K_PASS
ROW_BLOCKS = ROWS // P
BANK = 512
COL_BLOCKS = N // BANK

X_PARTS = (2, 2, 1, 2, 1, 1, 1, 1)
W_PARTS = (2, 2, 2, 4)

FLOPS = 2 * ROWS * K * N


def tile_sparselinearrelu_kernel(tc, x, weight_words, weight_scales, bias, out):
    nc = tc.nc
    relu = mybir.ActivationFunctionType.Relu
    with ExitStack() as stack:
        keep = stack.enter_context(tc.tile_pool(name="keep", bufs=1))
        work = stack.enter_context(tc.tile_pool(name="work", bufs=4))
        psum_t = stack.enter_context(tc.psum_pool(name="psum_t", bufs=4))
        psum_o = stack.enter_context(tc.psum_pool(name="psum_o", bufs=4))
        stack.enter_context(tc.manual_schedule())

        w_words = [
            [
                keep.tile([P, GROUPS // W_PARTS[c], 2 * BANK], U8, name="w_words%d_%d" % (c, h), align_bytes=64)
                for h in range(W_PARTS[c])
            ]
            for c in range(COL_BLOCKS)
        ]
        w_planes = [
            keep.tile([P, GROUPS, BANK], U8, name="w_planes%d" % c, align_bytes=64) for c in range(COL_BLOCKS)
        ]
        bias_rows = keep.tile([P, BANK], BF16)
        pick = keep.tile([P, COL_BLOCKS], BF16)
        bias_all = keep.tile([P, N], BF16)
        ones = keep.tile([P, BANK], BF16)
        ident = keep.tile([P, P], F32)
        warm = keep.tile([P, 1], F32)
        x_raw = [
            [keep.tile([P, K // X_PARTS[i]], BF16, name="x_raw%d_%d" % (i, h)) for h in range(X_PARTS[i])]
            for i in range(ROW_BLOCKS)
        ]
        x_codes = [
            keep.tile([P, GROUPS * P], U32, name="x_codes%d" % i, align_bytes=64) for i in range(ROW_BLOCKS)
        ]
        x_planes = [
            keep.tile([P, GROUPS * P], U8, name="x_planes%d" % i, align_bytes=64) for i in range(ROW_BLOCKS)
        ]
        x_sorted = {}
        grouped = {}
        banks = {}
        results = {}

        def load_x(i):
            width = K // X_PARTS[i]
            for h in range(X_PARTS[i]):
                nc.sync.dma_start(out=x_raw[i][h][:], in_=x[i * P : (i + 1) * P, h * width : (h + 1) * width])

        def load_w(c):
            cols = slice(2 * BANK * c, 2 * BANK * (c + 1))
            per = GROUPS // W_PARTS[c]
            for h in range(W_PARTS[c]):
                nc.sync.dma_start(
                    out=w_words[c][h][:].bitcast(I32),
                    in_=weight_words[per * h : per * (h + 1), :, cols].rearrange("g p b -> p g b").bitcast(I32),
                )

        def load_s(c):
            cols = slice(BANK * c, BANK * (c + 1))
            for r in range(4):
                nc.sync.dma_start(
                    out=w_planes[c][r:P:32, :, :].bitcast(I32),
                    in_=weight_scales[:, r:16:4, cols].rearrange("g q n -> q g n").bitcast(I32),
                )

        nc.vector.memset(bias_rows[:].bitcast(I32), 0)
        nc.vector.memset(warm[:], 0.0)
        nc.scalar.activation(out=warm[:], in_=warm[:], func=relu)
        nc.vector.memset(w_planes[0][:].bitcast(I32), 0)
        nc.vector.memset(w_planes[1][:].bitcast(I32), 0)
        nc.gpsimd.memset(ones[:], 1.0)
        make_identity(nc, ident[:])
        nc.vector.tensor_copy(out=pick[:], in_=ident[:, :COL_BLOCKS])
        for c in range(2, COL_BLOCKS):
            nc.vector.memset(w_planes[c][:].bitcast(I32), 0)

        load_x(0)
        nc.sync.dma_start(out=bias_rows[0:COL_BLOCKS, :], in_=bias.rearrange("(c n) -> c n", c=COL_BLOCKS))
        load_x(1)
        load_s(0)
        load_w(0)
        load_s(1)
        load_w(1)
        load_s(2)
        load_w(2)
        load_x(2)
        load_x(3)
        load_s(3)
        load_w(3)
        for i in range(4, ROW_BLOCKS):
            load_x(i)

        def sort_words(i):
            x_sorted[i] = work.tile([P, K // 2], F32, tag="sorted", name="sorted%d" % i)
            per = GROUPS // X_PARTS[i]
            words = K // 2 // X_PARTS[i]
            for h in range(X_PARTS[i]):
                nc.vector.tensor_copy(
                    out=x_sorted[i][:, h * words : (h + 1) * words]
                    .bitcast(I32)
                    .rearrange("p (g u c) -> p g u c", g=per, u=2),
                    in_=x_raw[i][h][:].bitcast(I32).rearrange("p (g c u) -> p g u c", g=per, u=2),
                )

        def spread_bias(c):
            nc.tensor.matmul(
                out=spread[c // 2][:, BANK * (c % 2) : BANK * (c % 2 + 1)],
                lhsT=pick[:, c : c + 1].to_broadcast([P, P]),
                rhs=bias_rows[:],
                start=True,
                stop=True,
            )

        def transposes(i):
            banks[i] = []
            for h in range(GROUPS // 2):
                xt = psum_t.tile([P, 2, 2, P], F32, tag="xt")
                banks[i].append(xt)
                for gg in range(2):
                    for u in range(2):
                        g = 2 * h + gg
                        if i in x_sorted:
                            src = x_sorted[i][:, (2 * g + u) * P : (2 * g + u + 1) * P]
                        else:
                            src = x_raw[i][h][:].bitcast(F32)[:, 2 * P * gg + u : 2 * P * (gg + 1) : 2]
                        nc.tensor.transpose(xt[:, gg, u, :], src, ident[:])
                if i < 2:
                    spread_bias(2 * i + h)
            grouped[i] = work.tile([P, K], BF16, tag="grouped", name="grouped%d" % i, align_bytes=64)

        def copy_out(i, h, copy):
            pairs = grouped[i][:].bitcast(F32).rearrange("p (g m u) -> p g m u", g=GROUPS, u=2)
            copy(out=pairs[:, 2 * h : 2 * h + 2, :, :], in_=banks[i][h][:].rearrange("p g u m -> p g m u"))

        def quantise(i, parts=(0,), of=1):
            width = GROUPS * P // of
            for n in parts:
                cols = slice(n * width, (n + 1) * width)
                nc.vector.quantize_mx(
                    out=x_codes[i][:, cols].bitcast(FP8X4),
                    scales=x_planes[i][:, cols],
                    in_=grouped[i][:, 4 * n * width : 4 * (n + 1) * width],
                )

        def w_part(c, g):
            per = GROUPS // W_PARTS[c]
            return w_words[c][g // per][:, g % per, :]

        def passes_and_bias(i, first, width):
            acc = psum_o.tile([P, width], F32, tag="acc")
            for g in range(GROUPS):
                nc.tensor.matmul_mx(
                    out=acc[:],
                    lhsT=x_codes[i][:, g * P : (g + 1) * P].bitcast(FP8X4),
                    lhsT_scale=x_planes[i][:, g * P : (g + 1) * P],
                    rhs=w_part(first // BANK, g)[:, 2 * (first % BANK) : 2 * (first % BANK + width)].bitcast(FP4X4),
                    rhs_scale=w_planes[first // BANK][:, g, first % BANK : first % BANK + width],
                    start=(g == 0),
                    stop=(g == GROUPS - 1),
                )
            cols = slice(first, first + width)
            nc.vector.tensor_tensor(
                out=results[i][:, cols], in0=acc[:], in1=bias_all[:, cols], op=mybir.AluOpType.add
            )

        def relu_store(i, first, width, store_first):
            cols = slice(first, first + width)
            nc.scalar.activation(out=results[i][:, cols], in_=results[i][:, cols], func=relu)
            if store_first is not None:
                span = slice(store_first, first + width)
                nc.sync.dma_start(out=out[i * P : (i + 1) * P, span], in_=results[i][:, span])

        idle = psum_o.tile([P, BANK], F32, tag="acc")
        for n in range(4):
            nc.tensor.matmul(out=idle[:], lhsT=ones[:, :P], rhs=ones[:], start=True, stop=True)
        spread = [psum_o.tile([P, 2 * BANK], BF16, tag="acc", name="spread%d" % h) for h in range(2)]
        transposes(0)
        copy_out(0, 0, nc.vector.tensor_copy)
        copy_out(0, 1, nc.scalar.copy)
        quantise(0, (0, 1), 2)
        transposes(1)
        copy_out(1, 0, nc.scalar.copy)
        quantise(1, (0,), 2)
        copy_out(1, 1, nc.vector.tensor_copy)
        quantise(1, (1,), 2)
        for h in range(2):
            copy = nc.scalar.copy if h == 0 else nc.vector.tensor_copy
            copy(out=bias_all[:, 2 * BANK * h : 2 * BANK * (h + 1)], in_=spread[h][:])

        for j in range(ROW_BLOCKS // 2):
            a = 2 * j + 2
            more = a < ROW_BLOCKS
            sort_at, run_at = ((3, 4), 5) if j == 0 else ((0, 1), 3)
            for i in (2 * j, 2 * j + 1):
                results[i] = work.tile([P, N], F32, tag="res", name="res%d" % i)
            for idx in range(2 * COL_BLOCKS):
                if more:
                    c, i = idx // 2, 2 * j + idx % 2
                else:
                    c, i = idx % COL_BLOCKS, 2 * j + idx // COL_BLOCKS
                first = BANK * c
                if not more and idx == 2 * COL_BLOCKS - 1:
                    for q in range(4):
                        passes_and_bias(i, first + P * q, P)
                        relu_store(i, first + P * q, P, first + P * (q - 1) if q % 2 == 1 else None)
                    continue
                passes_and_bias(i, first, BANK)
                if not more and i == ROW_BLOCKS - 1 and c == 2:
                    store_first = first
                elif c % 2 == 1:
                    store_first = first - BANK
                else:
                    store_first = None
                if more and idx == sort_at[0]:
                    sort_words(a)
                if more and idx == sort_at[1]:
                    sort_words(a + 1)
                if more and idx == run_at:
                    transposes(a)
                    transposes(a + 1)
                    copy_out(a, 0, nc.scalar.copy)
                    copy_out(a, 1, nc.scalar.copy)
                    relu_store(i, first, BANK, store_first)
                    copy_out(a + 1, 0, nc.scalar.copy)
                    copy_out(a + 1, 1, nc.scalar.copy)
                    quantise(a)
                    continue
                if more and idx == run_at + 1:
                    quantise(a + 1)
                relu_store(i, first, BANK, store_first)
